import numpy as np
import ml_dtypes


def mxq(x, axis, fmt="e4m3"):
    dtype, down = {"e4m3": (ml_dtypes.float8_e4m3fn, 7), "e5m2": (ml_dtypes.float8_e5m2, 14)}[fmt]
    v = np.moveaxis(np.asarray(x, np.float32).astype(ml_dtypes.bfloat16).astype(np.float64), axis, -1)
    blocks = v.reshape(v.shape[:-1] + (-1, 32))
    amax = np.abs(blocks).max(-1, keepdims=True)
    byte = np.maximum(np.where(amax > 0, np.frexp(amax)[1] - 1 + 127, 0) - down, 1)
    scale = np.exp2(byte - 127.0)
    codes = (blocks / scale).astype(np.float32).astype(dtype).astype(np.float64)
    return np.moveaxis((codes * scale).reshape(v.shape), -1, axis)


WIDE = False


def mx_kscale(k):
    if not WIDE:
        return np.ones(k)
    levels = np.array([10, -10, 5, -5, 0])
    a = np.random.permutation(np.resize(levels, k // 512 * 4)).reshape(k // 512, 4)
    idx = np.arange(k)
    return np.exp2(a[idx // 512, idx % 128 // 32])


BF16 = ml_dtypes.bfloat16


def bf(x):
    return np.asarray(x, np.float32).astype(BF16)


def f64(x):
    return np.asarray(x).astype(np.float64)


B, NH, NW, C, K, P = 2, 16, 16, 1024, 256, 4
T = P * P
HAD = np.array([[1.0, 1.0, 1.0, 1.0],
                [1.0, -1.0, 1.0, -1.0],
                [1.0, 1.0, -1.0, -1.0],
                [1.0, -1.0, -1.0, 1.0]])


def setup_inputs():
    s = mx_kscale(C)
    return {"trans": bf(np.random.standard_normal((T, B, NH, NW, C)) * s),
            "weight": bf(np.random.standard_normal((T, C, K)) * 0.5 * P / np.sqrt(C) / s[:, None]),
            "bias": bf(np.random.standard_normal((1, 1, 1, K)) * 0.2)}


def reference(trans, weight, bias):
    x = f64(trans).reshape(T, B * NH * NW, C)
    y = mxq(x, 2, "e4m3") @ mxq(f64(weight), 1, "e4m3")
    y = y.reshape(P, P, B, NH, NW, K)
    r = np.stack([sum(HAD[p, u] * y[u] for u in range(P)) for p in range(P)])
    z = np.stack([sum(HAD[q, v] * r[:, v] for v in range(P)) for q in range(P)], axis=1) / T
    z = z.transpose(2, 3, 0, 4, 1, 5)
    return z.reshape(B, P * NH, P * NW, K) + f64(bias)

@@ -1,0 +1,231 @@
+from contextlib import ExitStack
+
+import concourse.mybir as mybir
+from concourse.masks import make_identity
+
+F32 = mybir.dt.float32
+BF16 = mybir.dt.bfloat16
+U32 = mybir.dt.uint32
+U8 = mybir.dt.uint8
+FP8X4 = mybir.dt.float8_e4m3fn_x4
+ALU = mybir.AluOpType
+
+P = 128
+N_OUT = 256
+STEPS = 16
+FLOPS = 2 * 16 * 512 * 1024 * 256
+
+PLUS = {1: (0, 2), 2: (0, 1), 3: (0, 3)}
+VECTOR_PIECES = {0: [0,2,4,6], 1: [0,4,6], 2: [0,4,6], 3: [0,4,6]}
+
+
+def tile_iwht3layer_pa_t_kernel(tc, trans, weight, bias, out):
+    nc = tc.nc
+    x_view = trans.rearrange("t b i (jj s) c -> (b i jj) t s c", s=4)
+    w_view = weight.rearrange("t (a q e) n -> q t a (e n)", a=4, q=P, e=2)
+    o_view = out.rearrange("b (i pp) (jj s q) n -> (b i) pp jj s (q n)", pp=4, jj=4, s=4, q=4)
+
+    with ExitStack() as ctx:
+        const = ctx.enter_context(tc.tile_pool(name="const", bufs=1))
+        wq_pool = ctx.enter_context(tc.tile_pool(name="wq", bufs=1))
+        wraw_pool = ctx.enter_context(tc.tile_pool(name="wraw", bufs=8))
+        wgrp_pool = ctx.enter_context(tc.tile_pool(name="wgrp", bufs=2))
+        xraw_pool = ctx.enter_context(tc.tile_pool(name="xraw", bufs=5))
+        xgrp_pool = ctx.enter_context(tc.tile_pool(name="xgrp", bufs=2))
+        xq_pool = ctx.enter_context(tc.tile_pool(name="xq", bufs=3))
+        r_pool = ctx.enter_context(tc.tile_pool(name="r", bufs=2))
+        am_pool = ctx.enter_context(tc.tile_pool(name="am", bufs=2))
+        z_pool = ctx.enter_context(tc.tile_pool(name="z", bufs=2))
+        ps_t = ctx.enter_context(tc.psum_pool(name="pst", bufs=4))
+        ps_a = ctx.enter_context(tc.psum_pool(name="psa", bufs=4))
+        ctx.enter_context(tc.manual_schedule())
+
+        ident = const.tile([P, P], F32)
+        make_identity(nc, ident[:])
+        bias_bc = const.tile([P, N_OUT], BF16)
+        nc.scalar.dma_start(out=bias_bc[:], in_=bias.rearrange("a b c n -> (a b c n)").partition_broadcast(P))
+        bias_f = const.tile([P, N_OUT], F32)
+        nc.gpsimd.tensor_copy(out=bias_f[:], in_=bias_bc[:])
+        wc = wq_pool.tile([P, 16 * 512], U32, align_bytes=64)
+        ws = wq_pool.tile([P, 16 * 512], U8, align_bytes=64)
+
+        xraw = {}
+        wraw = {}
+        xts = {}
+        xgrp = {}
+        xcs = {}
+        banks = {}
+        rs = {}
+        zs = {}
+
+        def load_x(k):
+            s, u = divmod(k, 4)
+            xr = xraw_pool.tile([P, 4096], BF16)
+            nc.sync.dma_start(out=xr[:].rearrange("p (v c) -> p v c", v=4), in_=x_view[:, 4 * u : 4 * u + 4, s, :])
+            xraw[k] = xr
+
+        def load_w(u):
+            for t in range(4 * u, 4 * u + 4):
+                wr = wraw_pool.tile([P, 2048], BF16)
+                nc.sync.dma_start(out=wr[:].rearrange("q (a m) -> q a m", a=4), in_=w_view[:, t, :, :])
+                wraw[t] = wr
+
+        def transposes(k):
+            xw = xraw[k][:].bitcast(F32)
+            tiles = []
+            for v in range(4):
+                xt = ps_t.tile([P, 512], F32)
+                for a in range(4):
+                    nc.tensor.transpose(xt[:, P * a : P * a + P], xw[:, 512 * v + P * a : 512 * v + P * a + P], ident[:])
+                tiles.append(xt)
+            xts[k] = tiles
+
+        def evacuate(k):
+            xg = xgrp_pool.tile([P, 4096], BF16, align_bytes=64)
+            xgw = xg[:].bitcast(F32)
+            for v in range(4):
+                nc.scalar.copy(
+                    out=xgw[:, 512 * v : 512 * v + 512].rearrange("q (g p u) -> q g p u", g=2, p=P, u=2),
+                    in_=xts[k][v][:].rearrange("q (g u p) -> q g p u", g=2, u=2, p=P),
+                )
+            xgrp[k] = xg
+
+        def quantise_x(k):
+            xc = xq_pool.tile([P, 1024], U32, align_bytes=64)
+            xs = xq_pool.tile([P, 1024], U8, align_bytes=64)
+            nc.vector.quantize_mx(out=xc[:].bitcast(FP8X4), scales=xs[:], in_=xgrp[k][:])
+            xcs[k] = (xc, xs)
+
+        def weights(u):
+            pending = None
+            for half in range(2):
+                wg = wgrp_pool.tile([P, 4096], BF16, align_bytes=64)
+                for i in range(4):
+                    piece = 4 * half + i
+                    t = 4 * u + piece // 2
+                    g = piece % 2
+                    copy = nc.vector.tensor_copy if piece in VECTOR_PIECES[u] else nc.scalar.copy
+                    copy(
+                        out=wg[:, 1024 * i : 1024 * i + 1024].rearrange("q (c i j) -> q c j i", c=64, i=4, j=4),
+                        in_=wraw[t][:, 1024 * g : 1024 * g + 1024].rearrange("q (j c i) -> q c j i", j=4, c=64, i=4),
+                    )
+                if pending is not None:
+                    quantise_w(pending[0], pending[1])
+                pending = (2 * u + half, wg)
+            quantise_w(pending[0], pending[1])
+
+        def quantise_w(pair, wg):
+            nc.vector.quantize_mx(
+                out=wc[:, 1024 * pair : 1024 * pair + 1024].bitcast(FP8X4), scales=ws[:, 1024 * pair : 1024 * pair + 1024], in_=wg[:]
+            )
+
+        def sums(k):
+            u = k % 4
+            xc, xs = xcs[k]
+            bank_x = ps_a.tile([P, 512], F32, tag="acc")
+            bank_y = ps_a.tile([P, 512], F32, tag="acc")
+            jobs = [(bank_x, 0, (0, 1, 2, 3)), (bank_x, 1, PLUS[1]), (bank_y, 0, PLUS[2]), (bank_y, 1, PLUS[3])]
+            for bank, half, members in jobs:
+                passes = [(v, g) for v in members for g in range(2)]
+                for i, (v, g) in enumerate(passes):
+                    xo = (2 * v + g) * P
+                    wo = (2 * (4 * u + v) + g) * N_OUT
+                    nc.tensor.matmul_mx(
+                        out=bank[:, N_OUT * half : N_OUT * half + N_OUT],
+                        lhsT=xc[:, xo : xo + P].bitcast(FP8X4),
+                        lhsT_scale=xs[:, xo : xo + P],
+                        rhs=wc[:, wo : wo + N_OUT].bitcast(FP8X4),
+                        rhs_scale=ws[:, wo : wo + N_OUT],
+                        start=(i == 0),
+                        stop=(i == len(passes) - 1),
+                    )
+            banks[k] = (bank_x, bank_y)
+
+        def halves(ap):
+            return ap.rearrange("p (h n) -> p h n", h=2)
+
+        def level1(k):
+            s, u = divmod(k, 4)
+            bank_x, bank_y = banks[k]
+            if u == 0:
+                r_new = r_pool.tile([P, 4096], F32)
+                rs[s] = r_new
+            r = rs[s][:, 1024 * u : 1024 * u + 1024]
+            nc.scalar.mul(out=r[:, 0:N_OUT], in_=bank_x[:, 0:N_OUT], mul=1.0 / 16.0)
+            base = r[:, 0:N_OUT]
+            if u == 0:
+                am = am_pool.tile([P, N_OUT], F32)
+                nc.gpsimd.tensor_tensor(out=am[:], in0=r[:, 0:N_OUT], in1=bias_f[:], op=ALU.subtract)
+                nc.gpsimd.tensor_tensor(out=r[:, 0:N_OUT], in0=r[:, 0:N_OUT], in1=bias_f[:], op=ALU.add)
+                base = am[:]
+            nc.vector.scalar_tensor_tensor(
+                out=r[:, N_OUT:512], in0=bank_x[:, N_OUT:512], scalar=0.125, in1=base, op0=ALU.mult, op1=ALU.subtract
+            )
+            nc.vector.scalar_tensor_tensor(
+                out=halves(r[:, 512:1024]), in0=halves(bank_y[:]), scalar=0.125,
+                in1=base.unsqueeze(1).to_broadcast([P, 2, N_OUT]), op0=ALU.mult, op1=ALU.subtract,
+            )
+
+        def pair_stage(s, h):
+            if h == 0:
+                z_new = z_pool.tile([P, 4096], F32)
+                zs[s] = z_new
+            lo = 2048 * h
+            r = rs[s]
+            z = zs[s]
+            nc.vector.tensor_tensor(out=z[:, lo : lo + 1024], in0=r[:, lo : lo + 1024], in1=r[:, lo + 1024 : lo + 2048], op=ALU.add)
+            nc.vector.tensor_tensor(
+                out=z[:, lo + 1024 : lo + 2048], in0=r[:, lo : lo + 1024], in1=r[:, lo + 1024 : lo + 2048], op=ALU.subtract
+            )
+
+        def finish(s, h):
+            r = rs[s]
+            z = zs[s]
+            lo = 2048 * h
+            nc.vector.tensor_tensor(
+                out=r[:, lo : lo + 2048], in0=z[:, 0:2048], in1=z[:, 2048:4096], op=(ALU.add if h == 0 else ALU.subtract)
+            )
+            for jj in range(4):
+                nc.sync.dma_start(
+                    out=o_view[:, 2 * h : 2 * h + 2, jj, s, :],
+                    in_=r[jj:P:4, lo : lo + 2048].rearrange("p (m c) -> p m c", m=2),
+                )
+
+        load_w(0)
+        load_x(0)
+        load_x(1)
+        load_w(1)
+        load_x(2)
+
+        weights(0)
+        load_w(2)
+        load_x(3)
+        for k in range(-1, STEPS):
+            nxt = k + 1
+            if nxt < STEPS:
+                transposes(nxt)
+                evacuate(nxt)
+            if k >= 0:
+                sums(k)
+            if nxt < STEPS:
+                quantise_x(nxt)
+            if k >= 0:
+                s, u = divmod(k, 4)
+                level1(k)
+                if u == 0 and s >= 1:
+                    finish(s - 1, 0)
+                if u == 1:
+                    pair_stage(s, 0)
+                if u == 2 and s >= 1:
+                    finish(s - 1, 1)
+                if u == 3:
+                    pair_stage(s, 1)
+            if 1 <= nxt < 4:
+                weights(nxt)
+            if nxt == 1:
+                load_w(3)
+                load_x(4)
+            if 1 <= nxt and nxt + 4 < STEPS:
+                load_x(nxt + 4)
+        finish(3, 0)
+        finish(3, 1)

@@ -16,7 +16,6 @@ STEPS = 16
 FLOPS = 2 * 16 * 512 * 1024 * 256
 
 PLUS = {1: (0, 2), 2: (0, 1), 3: (0, 3)}
-VECTOR_PIECES = {0: [0,2,4,6], 1: [0,4,6], 2: [0,4,6], 3: [0,4,6]}
 
 
 def tile_iwht3layer_pa_t_kernel(tc, trans, weight, bias, out):
@@ -100,14 +99,15 @@ def tile_iwht3layer_pa_t_kernel(tc, trans, weight, bias, out):
             pending = None
             for half in range(2):
                 wg = wgrp_pool.tile([P, 4096], BF16, align_bytes=64)
-                for i in range(4):
-                    piece = 4 * half + i
-                    t = 4 * u + piece // 2
-                    g = piece % 2
-                    copy = nc.vector.tensor_copy if piece in VECTOR_PIECES[u] else nc.scalar.copy
-                    copy(
-                        out=wg[:, 1024 * i : 1024 * i + 1024].rearrange("q (c i j) -> q c j i", c=64, i=4, j=4),
-                        in_=wraw[t][:, 1024 * g : 1024 * g + 1024].rearrange("q (j c i) -> q c j i", j=4, c=64, i=4),
+                t = 4 * u + 2 * half
+                nc.vector.tensor_copy(
+                    out=wg[:, 0:2048].rearrange("q (g c i j) -> q g c j i", g=2, c=64, i=4, j=4),
+                    in_=wraw[t][:].rearrange("q (g j c i) -> q g c j i", g=2, j=4, c=64, i=4),
+                )
+                for g in range(2):
+                    nc.scalar.copy(
+                        out=wg[:, 2048 + 1024 * g : 3072 + 1024 * g].rearrange("q (c i j) -> q c j i", c=64, i=4, j=4),
+                        in_=wraw[t + 1][:, 1024 * g : 1024 * g + 1024].rearrange("q (j c i) -> q c j i", j=4, c=64, i=4),
                     )
                 if pending is not None:
                     quantise_w(pending[0], pending[1])
@@ -191,41 +191,49 @@ def tile_iwht3layer_pa_t_kernel(tc, trans, weight, bias, out):
                     in_=r[jj:P:4, lo : lo + 2048].rearrange("p (m c) -> p m c", m=2),
                 )
 
-        load_w(0)
+        later = []
+        served = [0]
+
+        def second_level():
+            if served[0] < len(later):
+                job = later[served[0]]
+                served[0] += 1
+                job[0](job[1], job[2])
+
         load_x(0)
+        load_w(0)
         load_x(1)
         load_w(1)
         load_x(2)
-
+        transposes(0)
+        evacuate(0)
+        quantise_x(0)
         weights(0)
         load_w(2)
         load_x(3)
-        for k in range(-1, STEPS):
+        for k in range(STEPS):
+            s, u = divmod(k, 4)
             nxt = k + 1
             if nxt < STEPS:
                 transposes(nxt)
                 evacuate(nxt)
-            if k >= 0:
-                sums(k)
-            if nxt < STEPS:
                 quantise_x(nxt)
-            if k >= 0:
-                s, u = divmod(k, 4)
-                level1(k)
-                if u == 0 and s >= 1:
-                    finish(s - 1, 0)
-                if u == 1:
-                    pair_stage(s, 0)
-                if u == 2 and s >= 1:
-                    finish(s - 1, 1)
-                if u == 3:
-                    pair_stage(s, 1)
-            if 1 <= nxt < 4:
+            sums(k)
+            if nxt < 4:
                 weights(nxt)
             if nxt == 1:
                 load_w(3)
                 load_x(4)
-            if 1 <= nxt and nxt + 4 < STEPS:
+            level1(k)
+            if u == 1:
+                later.append((pair_stage, s, 0))
+            if u == 3:
+                later.append((pair_stage, s, 1))
+                later.append((finish, s, 0))
+                later.append((finish, s, 1))
+            if k >= 3:
+                second_level()
+            if nxt + 4 < STEPS:
                 load_x(nxt + 4)
-        finish(3, 0)
-        finish(3, 1)
+        for i in range(len(later) - served[0]):
+            second_level()

@@ -100,15 +100,15 @@ def tile_iwht3layer_pa_t_kernel(tc, trans, weight, bias, out):
             for half in range(2):
                 wg = wgrp_pool.tile([P, 4096], BF16, align_bytes=64)
                 t = 4 * u + 2 * half
-                nc.vector.tensor_copy(
-                    out=wg[:, 0:2048].rearrange("q (g c i j) -> q g c j i", g=2, c=64, i=4, j=4),
-                    in_=wraw[t][:].rearrange("q (g j c i) -> q g c j i", g=2, j=4, c=64, i=4),
-                )
                 for g in range(2):
                     nc.scalar.copy(
-                        out=wg[:, 2048 + 1024 * g : 3072 + 1024 * g].rearrange("q (c i j) -> q c j i", c=64, i=4, j=4),
-                        in_=wraw[t + 1][:, 1024 * g : 1024 * g + 1024].rearrange("q (j c i) -> q c j i", j=4, c=64, i=4),
+                        out=wg[:, 1024 * g : 1024 * g + 1024].rearrange("q (c i j) -> q c j i", c=64, i=4, j=4),
+                        in_=wraw[t][:, 1024 * g : 1024 * g + 1024].rearrange("q (j c i) -> q c j i", j=4, c=64, i=4),
                     )
+                nc.vector.tensor_copy(
+                    out=wg[:, 2048:4096].rearrange("q (g c i j) -> q g c j i", g=2, c=64, i=4, j=4),
+                    in_=wraw[t + 1][:].rearrange("q (g j c i) -> q g c j i", g=2, j=4, c=64, i=4),
+                )
                 if pending is not None:
                     quantise_w(pending[0], pending[1])
                 pending = (2 * u + half, wg)
@@ -181,15 +181,21 @@ def tile_iwht3layer_pa_t_kernel(tc, trans, weight, bias, out):
         def finish(s, h):
             r = rs[s]
             z = zs[s]
-            lo = 2048 * h
-            nc.vector.tensor_tensor(
-                out=r[:, lo : lo + 2048], in0=z[:, 0:2048], in1=z[:, 2048:4096], op=(ALU.add if h == 0 else ALU.subtract)
-            )
-            for jj in range(4):
-                nc.sync.dma_start(
-                    out=o_view[:, 2 * h : 2 * h + 2, jj, s, :],
-                    in_=r[jj:P:4, lo : lo + 2048].rearrange("p (m c) -> p m c", m=2),
+            parts = 2 if (s, h) == (3, 1) else 1
+            rows = 2 // parts
+            for part in range(parts):
+                zo = 1024 * rows * part
+                lo = 2048 * h + zo
+                nc.vector.tensor_tensor(
+                    out=r[:, lo : lo + 1024 * rows], in0=z[:, zo : zo + 1024 * rows], in1=z[:, 2048 + zo : 2048 + zo + 1024 * rows],
+                    op=(ALU.add if h == 0 else ALU.subtract),
                 )
+                pp = 2 * h + rows * part
+                for jj in range(4):
+                    nc.sync.dma_start(
+                        out=o_view[:, pp : pp + rows, jj, s, :],
+                        in_=r[jj:P:4, lo : lo + 1024 * rows].rearrange("p (m c) -> p m c", m=rows),
+                    )
 
         later = []
         served = [0]
@@ -231,7 +237,7 @@ def tile_iwht3layer_pa_t_kernel(tc, trans, weight, bias, out):
                 later.append((pair_stage, s, 1))
                 later.append((finish, s, 0))
                 later.append((finish, s, 1))
-            if k >= 3:
+            if k >= 1:
                 second_level()
             if nxt + 4 < STEPS:
                 load_x(nxt + 4)

@@ -56,6 +56,7 @@ def tile_iwht3layer_pa_t_kernel(tc, trans, weight, bias, out):
         banks = {}
         rs = {}
         zs = {}
+        bases = {}
 
         def load_x(k):
             s, u = divmod(k, 4)
@@ -144,20 +145,26 @@ def tile_iwht3layer_pa_t_kernel(tc, trans, weight, bias, out):
         def halves(ap):
             return ap.rearrange("p (h n) -> p h n", h=2)
 
-        def level1(k):
+        def level1_base(k):
             s, u = divmod(k, 4)
-            bank_x, bank_y = banks[k]
+            bank_x = banks[k][0]
             if u == 0:
                 r_new = r_pool.tile([P, 4096], F32)
                 rs[s] = r_new
             r = rs[s][:, 1024 * u : 1024 * u + 1024]
             nc.scalar.mul(out=r[:, 0:N_OUT], in_=bank_x[:, 0:N_OUT], mul=1.0 / 16.0)
-            base = r[:, 0:N_OUT]
+            bases[k] = r[:, 0:N_OUT]
             if u == 0:
                 am = am_pool.tile([P, N_OUT], F32)
                 nc.gpsimd.tensor_tensor(out=am[:], in0=r[:, 0:N_OUT], in1=bias_f[:], op=ALU.subtract)
                 nc.gpsimd.tensor_tensor(out=r[:, 0:N_OUT], in0=r[:, 0:N_OUT], in1=bias_f[:], op=ALU.add)
-                base = am[:]
+                bases[k] = am[:]
+
+        def level1(k):
+            s, u = divmod(k, 4)
+            bank_x, bank_y = banks[k]
+            r = rs[s][:, 1024 * u : 1024 * u + 1024]
+            base = bases[k]
             nc.vector.scalar_tensor_tensor(
                 out=r[:, N_OUT:512], in0=bank_x[:, N_OUT:512], scalar=0.125, in1=base, op0=ALU.mult, op1=ALU.subtract
             )
@@ -201,10 +208,12 @@ def tile_iwht3layer_pa_t_kernel(tc, trans, weight, bias, out):
         served = [0]
 
         def second_level():
-            if served[0] < len(later):
-                job = later[served[0]]
-                served[0] += 1
-                job[0](job[1], job[2])
+            if served[0] == len(later):
+                return False
+            job = later[served[0]]
+            served[0] += 1
+            job[0](job[1], job[2])
+            return True
 
         load_x(0)
         load_w(0)
@@ -230,6 +239,8 @@ def tile_iwht3layer_pa_t_kernel(tc, trans, weight, bias, out):
             if nxt == 1:
                 load_w(3)
                 load_x(4)
+            level1_base(k)
+            early = second_level()
             level1(k)
             if u == 1:
                 later.append((pair_stage, s, 0))
@@ -237,7 +248,7 @@ def tile_iwht3layer_pa_t_kernel(tc, trans, weight, bias, out):
                 later.append((pair_stage, s, 1))
                 later.append((finish, s, 0))
                 later.append((finish, s, 1))
-            if k >= 1:
+            if not early:
                 second_level()
             if nxt + 4 < STEPS:
                 load_x(nxt + 4)

@@ -15,7 +15,7 @@ N_OUT = 256
 STEPS = 16
 FLOPS = 2 * 16 * 512 * 1024 * 256
 
-PLUS = {1: (0, 2), 2: (0, 1), 3: (0, 3)}
+SUMS = ((0, 2), (1, 3), (0, 1), (0, 3))
 
 
 def tile_iwht3layer_pa_t_kernel(tc, trans, weight, bias, out):
@@ -34,6 +34,7 @@ def tile_iwht3layer_pa_t_kernel(tc, trans, weight, bias, out):
         xq_pool = ctx.enter_context(tc.tile_pool(name="xq", bufs=3))
         r_pool = ctx.enter_context(tc.tile_pool(name="r", bufs=2))
         am_pool = ctx.enter_context(tc.tile_pool(name="am", bufs=2))
+        low_pool = ctx.enter_context(tc.tile_pool(name="low", bufs=2))
         z_pool = ctx.enter_context(tc.tile_pool(name="z", bufs=2))
         ps_t = ctx.enter_context(tc.psum_pool(name="pst", bufs=4))
         ps_a = ctx.enter_context(tc.psum_pool(name="psa", bufs=4))
@@ -125,7 +126,7 @@ def tile_iwht3layer_pa_t_kernel(tc, trans, weight, bias, out):
             xc, xs = xcs[k]
             bank_x = ps_a.tile([P, 512], F32, tag="acc")
             bank_y = ps_a.tile([P, 512], F32, tag="acc")
-            jobs = [(bank_x, 0, (0, 1, 2, 3)), (bank_x, 1, PLUS[1]), (bank_y, 0, PLUS[2]), (bank_y, 1, PLUS[3])]
+            jobs = [(bank_x, 0, SUMS[0]), (bank_x, 1, SUMS[1]), (bank_y, 0, SUMS[2]), (bank_y, 1, SUMS[3])]
             for bank, half, members in jobs:
                 passes = [(v, g) for v in members for g in range(2)]
                 for i, (v, g) in enumerate(passes):
@@ -151,22 +152,31 @@ def tile_iwht3layer_pa_t_kernel(tc, trans, weight, bias, out):
             if u == 0:
                 r_new = r_pool.tile([P, 4096], F32)
                 rs[s] = r_new
-            r = rs[s][:, 1024 * u : 1024 * u + 1024]
-            nc.scalar.mul(out=r[:, 0:N_OUT], in_=bank_x[:, 0:N_OUT], mul=1.0 / 16.0)
-            bases[k] = r[:, 0:N_OUT]
+            odd = am_pool.tile([P, 512], F32)
+            nc.scalar.mul(out=odd[:, 0:N_OUT], in_=bank_x[:, N_OUT:512], mul=1.0 / 16.0)
+            nc.scalar.mul(out=odd[:, N_OUT:512], in_=bank_x[:, N_OUT:512], mul=-1.0 / 16.0)
+            low = None
             if u == 0:
-                am = am_pool.tile([P, N_OUT], F32)
-                nc.gpsimd.tensor_tensor(out=am[:], in0=r[:, 0:N_OUT], in1=bias_f[:], op=ALU.subtract)
-                nc.gpsimd.tensor_tensor(out=r[:, 0:N_OUT], in0=r[:, 0:N_OUT], in1=bias_f[:], op=ALU.add)
-                bases[k] = am[:]
+                low = low_pool.tile([P, N_OUT], F32)
+                nc.gpsimd.tensor_tensor(out=low[:], in0=odd[:, 0:N_OUT], in1=bias_f[:], op=ALU.subtract)
+                nc.gpsimd.tensor_tensor(out=odd[:, 0:N_OUT], in0=odd[:, 0:N_OUT], in1=bias_f[:], op=ALU.add)
+                nc.gpsimd.tensor_tensor(out=odd[:, N_OUT:512], in0=odd[:, N_OUT:512], in1=bias_f[:], op=ALU.add)
+            bases[k] = (odd, low)
 
         def level1(k):
             s, u = divmod(k, 4)
             bank_x, bank_y = banks[k]
             r = rs[s][:, 1024 * u : 1024 * u + 1024]
-            base = bases[k]
+            odd, low = bases[k]
+            base = r[:, 0:N_OUT]
+            if u == 0:
+                nc.vector.scalar_tensor_tensor(
+                    out=low[:], in0=bank_x[:, 0:N_OUT], scalar=1.0 / 16.0, in1=low[:], op0=ALU.mult, op1=ALU.add
+                )
+                base = low[:]
             nc.vector.scalar_tensor_tensor(
-                out=r[:, N_OUT:512], in0=bank_x[:, N_OUT:512], scalar=0.125, in1=base, op0=ALU.mult, op1=ALU.subtract
+                out=halves(r[:, 0:512]), in0=bank_x[:, 0:N_OUT].unsqueeze(1).to_broadcast([P, 2, N_OUT]), scalar=1.0 / 16.0,
+                in1=halves(odd[:]), op0=ALU.mult, op1=ALU.add,
             )
             nc.vector.scalar_tensor_tensor(
                 out=halves(r[:, 512:1024]), in0=halves(bank_y[:]), scalar=0.125,

@@ -15,7 +15,8 @@ N_OUT = 256
 STEPS = 16
 FLOPS = 2 * 16 * 512 * 1024 * 256
 
-SUMS = ((0, 2), (1, 3), (0, 1), (0, 3))
+PLUS = {1: (0, 2), 2: (0, 1), 3: (0, 3)}
+MINUS_3 = (1, 2)
 
 
 def tile_iwht3layer_pa_t_kernel(tc, trans, weight, bias, out):
@@ -34,7 +35,6 @@ def tile_iwht3layer_pa_t_kernel(tc, trans, weight, bias, out):
         xq_pool = ctx.enter_context(tc.tile_pool(name="xq", bufs=3))
         r_pool = ctx.enter_context(tc.tile_pool(name="r", bufs=2))
         am_pool = ctx.enter_context(tc.tile_pool(name="am", bufs=2))
-        low_pool = ctx.enter_context(tc.tile_pool(name="low", bufs=2))
         z_pool = ctx.enter_context(tc.tile_pool(name="z", bufs=2))
         ps_t = ctx.enter_context(tc.psum_pool(name="pst", bufs=4))
         ps_a = ctx.enter_context(tc.psum_pool(name="psa", bufs=4))
@@ -58,6 +58,8 @@ def tile_iwht3layer_pa_t_kernel(tc, trans, weight, bias, out):
         rs = {}
         zs = {}
         bases = {}
+        pair_bases = {}
+        shared = {}
 
         def load_x(k):
             s, u = divmod(k, 4)
@@ -121,78 +123,91 @@ def tile_iwht3layer_pa_t_kernel(tc, trans, weight, bias, out):
                 out=wc[:, 1024 * pair : 1024 * pair + 1024].bitcast(FP8X4), scales=ws[:, 1024 * pair : 1024 * pair + 1024], in_=wg[:]
             )
 
+        def accumulate(region, members, start, stop):
+            passes = [(step, v, g) for step, v in members for g in range(2)]
+            for i, (step, v, g) in enumerate(passes):
+                xc, xs = xcs[step]
+                xo = (2 * v + g) * P
+                wo = (2 * (4 * (step % 4) + v) + g) * N_OUT
+                nc.tensor.matmul_mx(
+                    out=region,
+                    lhsT=xc[:, xo : xo + P].bitcast(FP8X4),
+                    lhsT_scale=xs[:, xo : xo + P],
+                    rhs=wc[:, wo : wo + N_OUT].bitcast(FP8X4),
+                    rhs_scale=ws[:, wo : wo + N_OUT],
+                    start=(start and i == 0),
+                    stop=(stop and i == len(passes) - 1),
+                )
+
         def sums(k):
-            u = k % 4
-            xc, xs = xcs[k]
-            bank_x = ps_a.tile([P, 512], F32, tag="acc")
-            bank_y = ps_a.tile([P, 512], F32, tag="acc")
-            jobs = [(bank_x, 0, SUMS[0]), (bank_x, 1, SUMS[1]), (bank_y, 0, SUMS[2]), (bank_y, 1, SUMS[3])]
-            for bank, half, members in jobs:
-                passes = [(v, g) for v in members for g in range(2)]
-                for i, (v, g) in enumerate(passes):
-                    xo = (2 * v + g) * P
-                    wo = (2 * (4 * u + v) + g) * N_OUT
-                    nc.tensor.matmul_mx(
-                        out=bank[:, N_OUT * half : N_OUT * half + N_OUT],
-                        lhsT=xc[:, xo : xo + P].bitcast(FP8X4),
-                        lhsT_scale=xs[:, xo : xo + P],
-                        rhs=wc[:, wo : wo + N_OUT].bitcast(FP8X4),
-                        rhs_scale=ws[:, wo : wo + N_OUT],
-                        start=(i == 0),
-                        stop=(i == len(passes) - 1),
-                    )
-            banks[k] = (bank_x, bank_y)
+            first = k % 2 == 0
+            if first:
+                bank_all = ps_a.tile([P, 512], F32, tag="acc")
+                bank_two = ps_a.tile([P, 512], F32, tag="acc")
+                bank_mix = ps_a.tile([P, 512], F32, tag="acc")
+                shared[k // 2] = (bank_all, bank_mix)
+            else:
+                bank_two = ps_a.tile([P, 512], F32, tag="acc")
+                bank_all, bank_mix = shared[k // 2]
+            side = 0 if first else N_OUT
+            accumulate(bank_all[:, side : side + N_OUT], [(k, v) for v in range(4)], True, True)
+            accumulate(bank_two[:, 0:N_OUT], [(k, v) for v in PLUS[1]], True, True)
+            accumulate(bank_two[:, N_OUT:512], [(k, v) for v in PLUS[2]], True, True)
+            accumulate(bank_mix[:, 0:N_OUT], [(k, v) for v in PLUS[3]], first, not first)
+            if not first:
+                accumulate(
+                    bank_mix[:, N_OUT:512], [(k - 1, v) for v in PLUS[3]] + [(k, v) for v in MINUS_3], True, True
+                )
+            banks[k] = (bank_all, bank_two, bank_mix)
 
         def halves(ap):
             return ap.rearrange("p (h n) -> p h n", h=2)
 
         def level1_base(k):
             s, u = divmod(k, 4)
-            bank_x = banks[k][0]
+            bank_all = banks[k][0]
+            side = N_OUT * (u % 2)
             if u == 0:
                 r_new = r_pool.tile([P, 4096], F32)
                 rs[s] = r_new
-            odd = am_pool.tile([P, 512], F32)
-            nc.scalar.mul(out=odd[:, 0:N_OUT], in_=bank_x[:, N_OUT:512], mul=1.0 / 16.0)
-            nc.scalar.mul(out=odd[:, N_OUT:512], in_=bank_x[:, N_OUT:512], mul=-1.0 / 16.0)
-            low = None
+            r = rs[s][:, 1024 * u : 1024 * u + 1024]
+            nc.scalar.mul(out=r[:, 0:N_OUT], in_=bank_all[:, side : side + N_OUT], mul=1.0 / 16.0)
+            bases[k] = r[:, 0:N_OUT]
             if u == 0:
-                low = low_pool.tile([P, N_OUT], F32)
-                nc.gpsimd.tensor_tensor(out=low[:], in0=odd[:, 0:N_OUT], in1=bias_f[:], op=ALU.subtract)
-                nc.gpsimd.tensor_tensor(out=odd[:, 0:N_OUT], in0=odd[:, 0:N_OUT], in1=bias_f[:], op=ALU.add)
-                nc.gpsimd.tensor_tensor(out=odd[:, N_OUT:512], in0=odd[:, N_OUT:512], in1=bias_f[:], op=ALU.add)
-            bases[k] = (odd, low)
+                am = am_pool.tile([P, N_OUT], F32)
+                nc.gpsimd.tensor_tensor(out=am[:], in0=r[:, 0:N_OUT], in1=bias_f[:], op=ALU.subtract)
+                nc.gpsimd.tensor_tensor(out=r[:, 0:N_OUT], in0=r[:, 0:N_OUT], in1=bias_f[:], op=ALU.add)
+                bases[k] = am[:]
+            if u % 2 == 1:
+                both = am_pool.tile([P, N_OUT], F32)
+                nc.gpsimd.tensor_tensor(out=both[:], in0=bases[k - 1], in1=r[:, 0:N_OUT], op=ALU.add)
+                pair_bases[k] = both
 
         def level1(k):
             s, u = divmod(k, 4)
-            bank_x, bank_y = banks[k]
+            bank_two, bank_mix = banks[k][1], banks[k][2]
             r = rs[s][:, 1024 * u : 1024 * u + 1024]
-            odd, low = bases[k]
-            base = r[:, 0:N_OUT]
-            if u == 0:
-                nc.vector.scalar_tensor_tensor(
-                    out=low[:], in0=bank_x[:, 0:N_OUT], scalar=1.0 / 16.0, in1=low[:], op0=ALU.mult, op1=ALU.add
-                )
-                base = low[:]
             nc.vector.scalar_tensor_tensor(
-                out=halves(r[:, 0:512]), in0=bank_x[:, 0:N_OUT].unsqueeze(1).to_broadcast([P, 2, N_OUT]), scalar=1.0 / 16.0,
-                in1=halves(odd[:]), op0=ALU.mult, op1=ALU.add,
+                out=halves(r[:, N_OUT:768]), in0=halves(bank_two[:]), scalar=0.125,
+                in1=bases[k].unsqueeze(1).to_broadcast([P, 2, N_OUT]), op0=ALU.mult, op1=ALU.subtract,
             )
-            nc.vector.scalar_tensor_tensor(
-                out=halves(r[:, 512:1024]), in0=halves(bank_y[:]), scalar=0.125,
-                in1=base.unsqueeze(1).to_broadcast([P, 2, N_OUT]), op0=ALU.mult, op1=ALU.subtract,
-            )
-
-        def pair_stage(s, h):
-            if h == 0:
+            if u == 1:
                 z_new = z_pool.tile([P, 4096], F32)
                 zs[s] = z_new
+            if u % 2 == 1:
+                lo = 2048 * (u // 2)
+                nc.vector.scalar_tensor_tensor(
+                    out=halves(zs[s][:, lo : lo + 2048])[:, :, 768:1024], in0=halves(bank_mix[:]), scalar=0.125,
+                    in1=pair_bases[k][:].unsqueeze(1).to_broadcast([P, 2, N_OUT]), op0=ALU.mult, op1=ALU.subtract,
+                )
+
+        def pair_stage(s, h):
             lo = 2048 * h
             r = rs[s]
             z = zs[s]
-            nc.vector.tensor_tensor(out=z[:, lo : lo + 1024], in0=r[:, lo : lo + 1024], in1=r[:, lo + 1024 : lo + 2048], op=ALU.add)
+            nc.vector.tensor_tensor(out=z[:, lo : lo + 768], in0=r[:, lo : lo + 768], in1=r[:, lo + 1024 : lo + 1792], op=ALU.add)
             nc.vector.tensor_tensor(
-                out=z[:, lo + 1024 : lo + 2048], in0=r[:, lo : lo + 1024], in1=r[:, lo + 1024 : lo + 2048], op=ALU.subtract
+                out=z[:, lo + 1024 : lo + 1792], in0=r[:, lo : lo + 768], in1=r[:, lo + 1024 : lo + 1792], op=ALU.subtract
             )
 
         def finish(s, h):

@@ -16,7 +16,6 @@ STEPS = 16
 FLOPS = 2 * 16 * 512 * 1024 * 256
 
 PLUS = {1: (0, 2), 2: (0, 1), 3: (0, 3)}
-MINUS_3 = (1, 2)
 
 
 def tile_iwht3layer_pa_t_kernel(tc, trans, weight, bias, out):
@@ -57,9 +56,6 @@ def tile_iwht3layer_pa_t_kernel(tc, trans, weight, bias, out):
         banks = {}
         rs = {}
         zs = {}
-        bases = {}
-        pair_bases = {}
-        shared = {}
 
         def load_x(k):
             s, u = divmod(k, 4)
@@ -100,7 +96,6 @@ def tile_iwht3layer_pa_t_kernel(tc, trans, weight, bias, out):
             xcs[k] = (xc, xs)
 
         def weights(u):
-            pending = None
             for half in range(2):
                 wg = wgrp_pool.tile([P, 4096], BF16, align_bytes=64)
                 t = 4 * u + 2 * half
@@ -113,101 +108,70 @@ def tile_iwht3layer_pa_t_kernel(tc, trans, weight, bias, out):
                     out=wg[:, 2048:4096].rearrange("q (g c i j) -> q g c j i", g=2, c=64, i=4, j=4),
                     in_=wraw[t + 1][:].rearrange("q (g j c i) -> q g c j i", g=2, j=4, c=64, i=4),
                 )
-                if pending is not None:
-                    quantise_w(pending[0], pending[1])
-                pending = (2 * u + half, wg)
-            quantise_w(pending[0], pending[1])
+                quantise_w(2 * u + half, wg)
 
         def quantise_w(pair, wg):
             nc.vector.quantize_mx(
                 out=wc[:, 1024 * pair : 1024 * pair + 1024].bitcast(FP8X4), scales=ws[:, 1024 * pair : 1024 * pair + 1024], in_=wg[:]
             )
 
-        def accumulate(region, members, start, stop):
-            passes = [(step, v, g) for step, v in members for g in range(2)]
-            for i, (step, v, g) in enumerate(passes):
-                xc, xs = xcs[step]
-                xo = (2 * v + g) * P
-                wo = (2 * (4 * (step % 4) + v) + g) * N_OUT
-                nc.tensor.matmul_mx(
-                    out=region,
-                    lhsT=xc[:, xo : xo + P].bitcast(FP8X4),
-                    lhsT_scale=xs[:, xo : xo + P],
-                    rhs=wc[:, wo : wo + N_OUT].bitcast(FP8X4),
-                    rhs_scale=ws[:, wo : wo + N_OUT],
-                    start=(start and i == 0),
-                    stop=(stop and i == len(passes) - 1),
-                )
-
         def sums(k):
-            first = k % 2 == 0
-            if first:
-                bank_all = ps_a.tile([P, 512], F32, tag="acc")
-                bank_two = ps_a.tile([P, 512], F32, tag="acc")
-                bank_mix = ps_a.tile([P, 512], F32, tag="acc")
-                shared[k // 2] = (bank_all, bank_mix)
-            else:
-                bank_two = ps_a.tile([P, 512], F32, tag="acc")
-                bank_all, bank_mix = shared[k // 2]
-            side = 0 if first else N_OUT
-            accumulate(bank_all[:, side : side + N_OUT], [(k, v) for v in range(4)], True, True)
-            accumulate(bank_two[:, 0:N_OUT], [(k, v) for v in PLUS[1]], True, True)
-            accumulate(bank_two[:, N_OUT:512], [(k, v) for v in PLUS[2]], True, True)
-            accumulate(bank_mix[:, 0:N_OUT], [(k, v) for v in PLUS[3]], first, not first)
-            if not first:
-                accumulate(
-                    bank_mix[:, N_OUT:512], [(k - 1, v) for v in PLUS[3]] + [(k, v) for v in MINUS_3], True, True
-                )
-            banks[k] = (bank_all, bank_two, bank_mix)
+            u = k % 4
+            xc, xs = xcs[k]
+            bank_x = ps_a.tile([P, 512], F32, tag="acc")
+            bank_y = ps_a.tile([P, 512], F32, tag="acc")
+            jobs = [(bank_x, 0, (0, 1, 2, 3)), (bank_x, 1, PLUS[1]), (bank_y, 0, PLUS[2]), (bank_y, 1, PLUS[3])]
+            for bank, half, members in jobs:
+                passes = [(v, g) for v in members for g in range(2)]
+                for i, (v, g) in enumerate(passes):
+                    xo = (2 * v + g) * P
+                    wo = (2 * (4 * u + v) + g) * N_OUT
+                    nc.tensor.matmul_mx(
+                        out=bank[:, N_OUT * half : N_OUT * half + N_OUT],
+                        lhsT=xc[:, xo : xo + P].bitcast(FP8X4),
+                        lhsT_scale=xs[:, xo : xo + P],
+                        rhs=wc[:, wo : wo + N_OUT].bitcast(FP8X4),
+                        rhs_scale=ws[:, wo : wo + N_OUT],
+                        start=(i == 0),
+                        stop=(i == len(passes) - 1),
+                    )
+            banks[k] = (bank_x, bank_y)
 
         def halves(ap):
             return ap.rearrange("p (h n) -> p h n", h=2)
 
-        def level1_base(k):
+        def level1(k):
             s, u = divmod(k, 4)
-            bank_all = banks[k][0]
-            side = N_OUT * (u % 2)
+            bank_x, bank_y = banks[k]
             if u == 0:
                 r_new = r_pool.tile([P, 4096], F32)
                 rs[s] = r_new
             r = rs[s][:, 1024 * u : 1024 * u + 1024]
-            nc.scalar.mul(out=r[:, 0:N_OUT], in_=bank_all[:, side : side + N_OUT], mul=1.0 / 16.0)
-            bases[k] = r[:, 0:N_OUT]
+            nc.scalar.mul(out=r[:, 0:N_OUT], in_=bank_x[:, 0:N_OUT], mul=1.0 / 16.0)
+            base = r[:, 0:N_OUT]
             if u == 0:
                 am = am_pool.tile([P, N_OUT], F32)
                 nc.gpsimd.tensor_tensor(out=am[:], in0=r[:, 0:N_OUT], in1=bias_f[:], op=ALU.subtract)
                 nc.gpsimd.tensor_tensor(out=r[:, 0:N_OUT], in0=r[:, 0:N_OUT], in1=bias_f[:], op=ALU.add)
-                bases[k] = am[:]
-            if u % 2 == 1:
-                both = am_pool.tile([P, N_OUT], F32)
-                nc.gpsimd.tensor_tensor(out=both[:], in0=bases[k - 1], in1=r[:, 0:N_OUT], op=ALU.add)
-                pair_bases[k] = both
-
-        def level1(k):
-            s, u = divmod(k, 4)
-            bank_two, bank_mix = banks[k][1], banks[k][2]
-            r = rs[s][:, 1024 * u : 1024 * u + 1024]
+                base = am[:]
             nc.vector.scalar_tensor_tensor(
-                out=halves(r[:, N_OUT:768]), in0=halves(bank_two[:]), scalar=0.125,
-                in1=bases[k].unsqueeze(1).to_broadcast([P, 2, N_OUT]), op0=ALU.mult, op1=ALU.subtract,
+                out=r[:, N_OUT:512], in0=bank_x[:, N_OUT:512], scalar=0.125, in1=base, op0=ALU.mult, op1=ALU.subtract
             )
-            if u == 1:
-                z_new = z_pool.tile([P, 4096], F32)
-                zs[s] = z_new
-            if u % 2 == 1:
-                lo = 2048 * (u // 2)
-                nc.vector.scalar_tensor_tensor(
-                    out=halves(zs[s][:, lo : lo + 2048])[:, :, 768:1024], in0=halves(bank_mix[:]), scalar=0.125,
-                    in1=pair_bases[k][:].unsqueeze(1).to_broadcast([P, 2, N_OUT]), op0=ALU.mult, op1=ALU.subtract,
-                )
+            nc.vector.scalar_tensor_tensor(
+                out=halves(r[:, 512:1024]), in0=halves(bank_y[:]), scalar=0.125,
+                in1=base.unsqueeze(1).to_broadcast([P, 2, N_OUT]), op0=ALU.mult, op1=ALU.subtract,
+            )
 
         def pair_stage(s, h):
+            if h == 0:
+                z_new = z_pool.tile([P, 4096], F32)
+                zs[s] = z_new
             lo = 2048 * h
             r = rs[s]
             z = zs[s]
-            nc.vector.tensor_tensor(out=z[:, lo : lo + 768], in0=r[:, lo : lo + 768], in1=r[:, lo + 1024 : lo + 1792], op=ALU.add)
+            nc.vector.tensor_tensor(out=z[:, lo : lo + 1024], in0=r[:, lo : lo + 1024], in1=r[:, lo + 1024 : lo + 2048], op=ALU.add)
             nc.vector.tensor_tensor(
-                out=z[:, lo + 1024 : lo + 1792], in0=r[:, lo : lo + 768], in1=r[:, lo + 1024 : lo + 1792], op=ALU.subtract
+                out=z[:, lo + 1024 : lo + 2048], in0=r[:, lo : lo + 1024], in1=r[:, lo + 1024 : lo + 2048], op=ALU.subtract
             )
 
         def finish(s, h):
@@ -233,12 +197,10 @@ def tile_iwht3layer_pa_t_kernel(tc, trans, weight, bias, out):
         served = [0]
 
         def second_level():
-            if served[0] == len(later):
-                return False
-            job = later[served[0]]
-            served[0] += 1
-            job[0](job[1], job[2])
-            return True
+            if served[0] < len(later):
+                job = later[served[0]]
+                served[0] += 1
+                job[0](job[1], job[2])
 
         load_x(0)
         load_w(0)
@@ -264,8 +226,6 @@ def tile_iwht3layer_pa_t_kernel(tc, trans, weight, bias, out):
             if nxt == 1:
                 load_w(3)
                 load_x(4)
-            level1_base(k)
-            early = second_level()
             level1(k)
             if u == 1:
                 later.append((pair_stage, s, 0))
@@ -273,7 +233,7 @@ def tile_iwht3layer_pa_t_kernel(tc, trans, weight, bias, out):
                 later.append((pair_stage, s, 1))
                 later.append((finish, s, 0))
                 later.append((finish, s, 1))
-            if not early:
+            if k >= 1:
                 second_level()
             if nxt + 4 < STEPS:
                 load_x(nxt + 4)

from contextlib import ExitStack

import concourse.mybir as mybir
from concourse.masks import make_identity

F32 = mybir.dt.float32
BF16 = mybir.dt.bfloat16
U32 = mybir.dt.uint32
U8 = mybir.dt.uint8
FP8X4 = mybir.dt.float8_e4m3fn_x4
ALU = mybir.AluOpType

P = 128
N_OUT = 256
STEPS = 16
FLOPS = 2 * 16 * 512 * 1024 * 256

PLUS = {1: (0, 2), 2: (0, 1), 3: (0, 3)}


def tile_iwht3layer_pa_t_kernel(tc, trans, weight, bias, out):
    nc = tc.nc
    x_view = trans.rearrange("t b i (jj s) c -> (b i jj) t s c", s=4)
    w_view = weight.rearrange("t (a q e) n -> q t a (e n)", a=4, q=P, e=2)
    o_view = out.rearrange("b (i pp) (jj s q) n -> (b i) pp jj s (q n)", pp=4, jj=4, s=4, q=4)

    with ExitStack() as ctx:
        const = ctx.enter_context(tc.tile_pool(name="const", bufs=1))
        wq_pool = ctx.enter_context(tc.tile_pool(name="wq", bufs=1))
        wraw_pool = ctx.enter_context(tc.tile_pool(name="wraw", bufs=8))
        wgrp_pool = ctx.enter_context(tc.tile_pool(name="wgrp", bufs=2))
        xraw_pool = ctx.enter_context(tc.tile_pool(name="xraw", bufs=5))
        xgrp_pool = ctx.enter_context(tc.tile_pool(name="xgrp", bufs=2))
        xq_pool = ctx.enter_context(tc.tile_pool(name="xq", bufs=3))
        r_pool = ctx.enter_context(tc.tile_pool(name="r", bufs=2))
        am_pool = ctx.enter_context(tc.tile_pool(name="am", bufs=2))
        z_pool = ctx.enter_context(tc.tile_pool(name="z", bufs=2))
        ps_t = ctx.enter_context(tc.psum_pool(name="pst", bufs=4))
        ps_a = ctx.enter_context(tc.psum_pool(name="psa", bufs=4))
        ctx.enter_context(tc.manual_schedule())

        ident = const.tile([P, P], F32)
        make_identity(nc, ident[:])
        bias_bc = const.tile([P, N_OUT], BF16)
        nc.scalar.dma_start(out=bias_bc[:], in_=bias.rearrange("a b c n -> (a b c n)").partition_broadcast(P))
        bias_f = const.tile([P, N_OUT], F32)
        nc.gpsimd.tensor_copy(out=bias_f[:], in_=bias_bc[:])
        wc = wq_pool.tile([P, 16 * 512], U32, align_bytes=64)
        ws = wq_pool.tile([P, 16 * 512], U8, align_bytes=64)

        xraw = {}
        wraw = {}
        xts = {}
        xgrp = {}
        xcs = {}
        banks = {}
        rs = {}
        zs = {}

        def load_x(k):
            s, u = divmod(k, 4)
            xr = xraw_pool.tile([P, 4096], BF16)
            nc.sync.dma_start(out=xr[:].rearrange("p (v c) -> p v c", v=4), in_=x_view[:, 4 * u : 4 * u + 4, s, :])
            xraw[k] = xr

        def load_w(u):
            for t in range(4 * u, 4 * u + 4):
                wr = wraw_pool.tile([P, 2048], BF16)
                nc.sync.dma_start(out=wr[:].rearrange("q (a m) -> q a m", a=4), in_=w_view[:, t, :, :])
                wraw[t] = wr

        def transposes(k):
            xw = xraw[k][:].bitcast(F32)
            tiles = []
            for v in range(4):
                xt = ps_t.tile([P, 512], F32)
                for a in range(4):
                    nc.tensor.transpose(xt[:, P * a : P * a + P], xw[:, 512 * v + P * a : 512 * v + P * a + P], ident[:])
                tiles.append(xt)
            xts[k] = tiles

        def evacuate(k):
            xg = xgrp_pool.tile([P, 4096], BF16, align_bytes=64)
            xgw = xg[:].bitcast(F32)
            for v in range(4):
                nc.scalar.copy(
                    out=xgw[:, 512 * v : 512 * v + 512].rearrange("q (g p u) -> q g p u", g=2, p=P, u=2),
                    in_=xts[k][v][:].rearrange("q (g u p) -> q g p u", g=2, u=2, p=P),
                )
            xgrp[k] = xg

        def quantise_x(k):
            xc = xq_pool.tile([P, 1024], U32, align_bytes=64)
            xs = xq_pool.tile([P, 1024], U8, align_bytes=64)
            nc.vector.quantize_mx(out=xc[:].bitcast(FP8X4), scales=xs[:], in_=xgrp[k][:])
            xcs[k] = (xc, xs)

        def weights(u):
            for half in range(2):
                wg = wgrp_pool.tile([P, 4096], BF16, align_bytes=64)
                t = 4 * u + 2 * half
                for g in range(2):
                    nc.scalar.copy(
                        out=wg[:, 1024 * g : 1024 * g + 1024].rearrange("q (c i j) -> q c j i", c=64, i=4, j=4),
                        in_=wraw[t][:, 1024 * g : 1024 * g + 1024].rearrange("q (j c i) -> q c j i", j=4, c=64, i=4),
                    )
                nc.vector.tensor_copy(
                    out=wg[:, 2048:4096].rearrange("q (g c i j) -> q g c j i", g=2, c=64, i=4, j=4),
                    in_=wraw[t + 1][:].rearrange("q (g j c i) -> q g c j i", g=2, j=4, c=64, i=4),
                )
                quantise_w(2 * u + half, wg)

        def quantise_w(pair, wg):
            nc.vector.quantize_mx(
                out=wc[:, 1024 * pair : 1024 * pair + 1024].bitcast(FP8X4), scales=ws[:, 1024 * pair : 1024 * pair + 1024], in_=wg[:]
            )

        def sums(k):
            u = k % 4
            xc, xs = xcs[k]
            bank_x = ps_a.tile([P, 512], F32, tag="acc")
            bank_y = ps_a.tile([P, 512], F32, tag="acc")
            jobs = [(bank_x, 0, (0, 1, 2, 3)), (bank_x, 1, PLUS[1]), (bank_y, 0, PLUS[2]), (bank_y, 1, PLUS[3])]
            for bank, half, members in jobs:
                passes = [(v, g) for v in members for g in range(2)]
                for i, (v, g) in enumerate(passes):
                    xo = (2 * v + g) * P
                    wo = (2 * (4 * u + v) + g) * N_OUT
                    nc.tensor.matmul_mx(
                        out=bank[:, N_OUT * half : N_OUT * half + N_OUT],
                        lhsT=xc[:, xo : xo + P].bitcast(FP8X4),
                        lhsT_scale=xs[:, xo : xo + P],
                        rhs=wc[:, wo : wo + N_OUT].bitcast(FP8X4),
                        rhs_scale=ws[:, wo : wo + N_OUT],
                        start=(i == 0),
                        stop=(i == len(passes) - 1),
                    )
            banks[k] = (bank_x, bank_y)

        def halves(ap):
            return ap.rearrange("p (h n) -> p h n", h=2)

        def level1(k):
            s, u = divmod(k, 4)
            bank_x, bank_y = banks[k]
            if u == 0:
                r_new = r_pool.tile([P, 4096], F32)
                rs[s] = r_new
            r = rs[s][:, 1024 * u : 1024 * u + 1024]
            nc.scalar.mul(out=r[:, 0:N_OUT], in_=bank_x[:, 0:N_OUT], mul=1.0 / 16.0)
            base = r[:, 0:N_OUT]
            if u == 0:
                am = am_pool.tile([P, N_OUT], F32)
                nc.gpsimd.tensor_tensor(out=am[:], in0=r[:, 0:N_OUT], in1=bias_f[:], op=ALU.subtract)
                nc.gpsimd.tensor_tensor(out=r[:, 0:N_OUT], in0=r[:, 0:N_OUT], in1=bias_f[:], op=ALU.add)
                base = am[:]
            nc.vector.scalar_tensor_tensor(
                out=r[:, N_OUT:512], in0=bank_x[:, N_OUT:512], scalar=0.125, in1=base, op0=ALU.mult, op1=ALU.subtract
            )
            nc.vector.scalar_tensor_tensor(
                out=halves(r[:, 512:1024]), in0=halves(bank_y[:]), scalar=0.125,
                in1=base.unsqueeze(1).to_broadcast([P, 2, N_OUT]), op0=ALU.mult, op1=ALU.subtract,
            )

        def pair_stage(s, h):
            if h == 0:
                z_new = z_pool.tile([P, 4096], F32)
                zs[s] = z_new
            lo = 2048 * h
            r = rs[s]
            z = zs[s]
            nc.vector.tensor_tensor(out=z[:, lo : lo + 1024], in0=r[:, lo : lo + 1024], in1=r[:, lo + 1024 : lo + 2048], op=ALU.add)
            nc.vector.tensor_tensor(
                out=z[:, lo + 1024 : lo + 2048], in0=r[:, lo : lo + 1024], in1=r[:, lo + 1024 : lo + 2048], op=ALU.subtract
            )

        def finish(s, h):
            r = rs[s]
            z = zs[s]
            parts = 2 if (s, h) == (3, 1) else 1
            rows = 2 // parts
            for part in range(parts):
                zo = 1024 * rows * part
                lo = 2048 * h + zo
                nc.vector.tensor_tensor(
                    out=r[:, lo : lo + 1024 * rows], in0=z[:, zo : zo + 1024 * rows], in1=z[:, 2048 + zo : 2048 + zo + 1024 * rows],
                    op=(ALU.add if h == 0 else ALU.subtract),
                )
                pp = 2 * h + rows * part
                for jj in range(4):
                    nc.sync.dma_start(
                        out=o_view[:, pp : pp + rows, jj, s, :],
                        in_=r[jj:P:4, lo : lo + 1024 * rows].rearrange("p (m c) -> p m c", m=rows),
                    )

        later = []
        served = [0]

        def second_level():
            if served[0] < len(later):
                job = later[served[0]]
                served[0] += 1
                job[0](job[1], job[2])

        load_x(0)
        load_w(0)
        load_x(1)
        load_w(1)
        load_x(2)
        transposes(0)
        evacuate(0)
        quantise_x(0)
        weights(0)
        load_w(2)
        load_x(3)
        for k in range(STEPS):
            s, u = divmod(k, 4)
            nxt = k + 1
            if nxt < STEPS:
                transposes(nxt)
                evacuate(nxt)
                quantise_x(nxt)
            sums(k)
            if nxt < 4:
                weights(nxt)
            if nxt == 1:
                load_w(3)
                load_x(4)
            level1(k)
            if u == 1:
                later.append((pair_stage, s, 0))
            if u == 3:
                later.append((pair_stage, s, 1))
                later.append((finish, s, 0))
                later.append((finish, s, 1))
            if k >= 1:
                second_level()
            if nxt + 4 < STEPS:
                load_x(nxt + 4)
        for i in range(len(later) - served[0]):
            second_level()
